import numpy as np
import ml_dtypes

BF16 = ml_dtypes.bfloat16


def bf(x):
    return np.asarray(x, np.float32).astype(BF16)


def f32(x):
    return np.asarray(x, np.float32)


def f64(x):
    return np.asarray(x).astype(np.float64)


def striped(idx):
    return np.tile(idx.reshape(-1, 16).T, (8, 1))


B, S, T, F, N, E, C1, C2 = 1024, 2048, 2, 768, 1536, 2, 256, 1024


def log_softmax(v):
    v = v - v.max(axis=-1, keepdims=True)
    return v - np.log(np.exp(v).sum(axis=-1, keepdims=True))


def setup_inputs():
    return {
        "d": f32(np.random.standard_normal((B, S))),
        "wc": bf(np.random.standard_normal((T, F, E)) / np.sqrt(F)),
        "bc": f32(np.arange(E) + 0.2 * np.random.standard_normal((T, E))),
        "w1": bf(np.random.standard_normal((T, F, C1)) / np.sqrt(F)),
        "b1": f32(0.5 * np.random.standard_normal((T, C1))),
        "w2": bf(np.concatenate([np.random.standard_normal((T, F, C2)) / np.sqrt(F), np.random.standard_normal((T, C1, C2)) / np.sqrt(C1)], axis=1)),
        "b2": f32(0.5 * np.random.standard_normal((T, C2))),
        "offs": striped(np.random.permutation(np.tile(np.arange(S), 2))[:N]),
    }


def reference(d, wc, bc, w1, b1, w2, b2, offs):
    idx = offs[:16].T.reshape(-1)
    x = f64(d)[:, idx]
    parts = []
    for t in range(T):
        xt = x[:, t * F:(t + 1) * F]
        z = (xt[:, :, None] * f64(wc)[t][None]).sum(axis=1) + f64(bc)[t]
        lw = log_softmax(z)[:, 1:]
        h = xt @ f64(w1)[t] + f64(b1)[t]
        u = xt @ f64(w2)[t, :F] + np.maximum(h, 0.0) @ f64(w2)[t, F:] + f64(b2)[t]
        parts.append(log_softmax(h) + lw)
        parts.append(log_softmax(u) + lw)
    return np.concatenate(parts, axis=1)

@@ -1,0 +1,194 @@
+import concourse.mybir as mybir
+from concourse.masks import make_identity
+
+F32, BF16, U16 = mybir.dt.float32, mybir.dt.bfloat16, mybir.dt.uint16
+ACT = mybir.ActivationFunctionType
+ALU = mybir.AluOpType
+X_AXIS = mybir.AxisListType.X
+
+P = 128
+B, S, T, F, E, C1, C2 = 1024, 2048, 2, 768, 2, 256, 1024
+UNITS = (B // P) * T
+KF = F // P
+KH = C1 // P
+BANK = 512
+FLIPS_IN_BANK = BANK // P
+HZ = C1 + E
+WIDTH = C1 + C2
+W1_ROW = C1 + 16
+B1_ROW = C1 + 8
+H_COL, U_COL, Z_COL = 0, 1, 2
+
+FLOPS = 2 * B * T * (F * (E + C1 + C2) + C1 * C2)
+
+
+def tile_forestclf_b_kernel(tc, d, wc, bc, w1, b1, w2, b2, offs, out):
+    nc = tc.nc
+    with (
+        tc.tile_pool(name="held", bufs=1) as held,
+        tc.tile_pool(name="windows", bufs=3) as windows,
+        tc.tile_pool(name="work", bufs=3) as work,
+        tc.psum_pool(name="psum_single", bufs=1) as psum_single,
+        tc.psum_pool(name="psum_double", bufs=2) as psum_double,
+    ):
+        offsets = held.tile([P, T * F // 16], U16, name="offsets")
+        nc.sync.dma_start(offsets[:], offs)
+
+        window = {}
+
+        def load_window(i):
+            window[i] = windows.tile([P, S], F32, name="window")
+            nc.sync.dma_start(window[i][:], d[i * P : (i + 1) * P, :])
+
+        w1c = held.tile([P, T, KF, W1_ROW], BF16, name="w1c")
+        b1c = held.tile([P, T, B1_ROW], F32, name="b1c")
+        b2_all = held.tile([P, T, C2], F32, name="b2_all")
+        for t in range(T):
+            nc.scalar.dma_start(w1c[:, t, :, 0:C1], w1[t, :, :].rearrange("(a p) c -> p a c", p=P))
+            nc.scalar.dma_start(w1c[:, t, :, C1:HZ], wc[t, :, :].rearrange("(a p) e -> p a e", p=P))
+            nc.scalar.dma_start(b1c[:, t, 0:C1], b1[t, :].partition_broadcast(P))
+            nc.scalar.dma_start(b1c[:, t, C1:HZ], bc[t, :].partition_broadcast(P))
+        for t in range(T):
+            nc.scalar.dma_start(b2_all[:, t, :], b2[t, :].partition_broadcast(P))
+
+        w2_rows = {}
+
+        def load_w2(t):
+            for a in range(KF + KH):
+                w2_rows[t, a] = held.tile([P, C2], BF16, name="w2_rows_%d_%d" % (t, a))
+                nc.sync.dma_start(w2_rows[t, a][:], w2[t, a * P : (a + 1) * P, :])
+
+        load_window(0)
+        load_w2(0)
+        load_window(1)
+        load_w2(1)
+        load_window(2)
+
+        ident_f32 = held.tile([P, P], F32, name="ident_f32")
+        make_identity(nc, ident_f32[:])
+        ident_bf16 = held.tile([P, P], BF16, name="ident_bf16")
+        make_identity(nc, ident_bf16[:])
+
+        picked, flipped, h_bank, hz, relu, relu_bank, relu_flipped = {}, {}, {}, {}, {}, {}, {}
+        u_bank, u_biased, neg_max, exp_sum, log_sum = {}, {}, {}, {}, {}
+
+        def gather(k):
+            i, t = divmod(k, T)
+            picked[k] = work.tile([P, F], F32, name="picked")
+            piece = offsets[:, t * (F // 16) : (t + 1) * (F // 16)]
+            nc.scalar.activation(picked[k][:], window[i][:].indirect(piece), ACT.Copy)
+            if t == T - 1 and i + 3 < B // P:
+                load_window(i + 3)
+
+        def flip(k):
+            flipped[k] = work.tile([P, KF, P], BF16, name="flipped")
+            for first in range(0, KF, FLIPS_IN_BANK):
+                count = min(FLIPS_IN_BANK, KF - first)
+                bank = psum_single.tile([P, count, P], F32, name="flip_bank_%d" % first)
+                for a in range(count):
+                    nc.tensor.transpose(bank[:, a, :], picked[k][:, (first + a) * P : (first + a + 1) * P], ident_f32[:])
+                nc.scalar.copy(flipped[k][:, first : first + count, :], bank[:])
+
+        def hidden_product(k):
+            t = k % T
+            h_bank[k] = psum_single.tile([P, HZ], F32, name="h_bank")
+            for a in range(KF):
+                nc.tensor.matmul(h_bank[k][:], lhsT=flipped[k][:, a, :], rhs=w1c[:, t, a, 0:HZ], start=(a == 0), stop=(a == KF - 1))
+
+        def hidden_bias(k):
+            t = k % T
+            hz[k] = work.tile([P, HZ], F32, name="hz")
+            nc.vector.tensor_tensor(hz[k][:], h_bank[k][:], b1c[:, t, 0:HZ], ALU.add)
+            relu[k] = work.tile([P, C1], BF16, name="relu")
+            nc.vector.tensor_scalar_max(relu[k][:], hz[k][:, 0:C1], 0.0)
+
+        def flip_relu(k):
+            relu_bank[k] = psum_single.tile([P, KH, P], BF16, name="relu_bank")
+            for a in range(KH):
+                nc.tensor.transpose(relu_bank[k][:, a, :], relu[k][:, a * P : (a + 1) * P], ident_bf16[:])
+
+        def copy_flipped_relu(k):
+            relu_flipped[k] = work.tile([P, KH, P], BF16, name="relu_flipped")
+            nc.vector.tensor_copy(relu_flipped[k][:], relu_bank[k][:])
+
+        def wide_product(k, row_blocks):
+            t = k % T
+            for a in row_blocks:
+                stationary = flipped[k][:, a, :] if a < KF else relu_flipped[k][:, a - KF, :]
+                for n in range(C2 // BANK):
+                    nc.tensor.matmul(
+                        u_bank[k, n][:], lhsT=stationary, rhs=w2_rows[t, a][:, n * BANK : (n + 1) * BANK],
+                        start=(a == 0), stop=(a == KF + KH - 1),
+                    )
+
+        def softmax_sum(k, col, values):
+            nc.vector.tensor_reduce(neg_max[k][:, col : col + 1], values, X_AXIS, ALU.max, negate=True)
+            unused = work.tile([P, C2], BF16, name="unused")
+            nc.scalar.activation(
+                unused[:, 0 : values.shape[1]], values, ACT.Exp,
+                bias=neg_max[k][:, col : col + 1], accum_out=exp_sum[k][:, col : col + 1],
+            )
+
+        def hidden_softmax_sums(k):
+            neg_max[k] = work.tile([P, 3], F32, name="neg_max")
+            exp_sum[k] = work.tile([P, 3], F32, name="exp_sum")
+            softmax_sum(k, H_COL, hz[k][:, 0:C1])
+            softmax_sum(k, Z_COL, hz[k][:, C1:HZ])
+
+        def wide_bias(k):
+            t = k % T
+            u_biased[k] = work.tile([P, C2], F32, name="u_biased")
+            for n in range(C2 // BANK):
+                cols = slice(n * BANK, (n + 1) * BANK)
+                nc.vector.tensor_tensor(u_biased[k][:, cols], u_bank[k, n][:], b2_all[:, t, cols], ALU.add)
+
+        def wide_softmax_sum(k):
+            softmax_sum(k, U_COL, u_biased[k][:])
+            log_sum[k] = work.tile([P, 3], F32, name="log_sum")
+            nc.scalar.activation(log_sum[k][:], exp_sum[k][:], ACT.Ln)
+
+        def finish(k):
+            i, t = divmod(k, T)
+            log_norm = work.tile([P, 3], F32, name="log_norm")
+            nc.vector.tensor_tensor(log_norm[:], log_sum[k][:], neg_max[k][:], ALU.subtract)
+            neg_lw = work.tile([P, 1], F32, name="neg_lw")
+            nc.vector.tensor_tensor(neg_lw[:], log_norm[:, Z_COL : Z_COL + 1], hz[k][:, C1 + 1 : C1 + 2], ALU.subtract)
+            result = work.tile([P, WIDTH], F32, name="result")
+            nc.vector.tensor_scalar(
+                result[:, 0:C1], hz[k][:, 0:C1], log_norm[:, H_COL : H_COL + 1], neg_lw[:], ALU.subtract, ALU.subtract
+            )
+            nc.vector.tensor_scalar(
+                result[:, C1:WIDTH], u_biased[k][:], log_norm[:, U_COL : U_COL + 1], neg_lw[:], ALU.subtract, ALU.subtract
+            )
+            nc.sync.dma_start(out[i * P : (i + 1) * P, t * WIDTH : (t + 1) * WIDTH], result[:])
+
+        gather(0)
+        flip(0)
+        gather(1)
+        hidden_product(0)
+        flip(1)
+        gather(2)
+        for k in range(UNITS):
+            for n in range(C2 // BANK):
+                u_bank[k, n] = psum_double.tile([P, BANK], F32, name="u_bank_%d" % n)
+            wide_product(k, range(0, KF // 2))
+            if k >= 1:
+                wide_bias(k - 1)
+            hidden_bias(k)
+            flip_relu(k)
+            if k >= 1:
+                wide_softmax_sum(k - 1)
+            hidden_softmax_sums(k)
+            if k + 3 < UNITS:
+                gather(k + 3)
+            copy_flipped_relu(k)
+            wide_product(k, range(KF // 2, KF + KH))
+            if k >= 1:
+                finish(k - 1)
+            if k + 1 < UNITS:
+                hidden_product(k + 1)
+            if k + 2 < UNITS:
+                flip(k + 2)
+        wide_bias(UNITS - 1)
+        wide_softmax_sum(UNITS - 1)
+        finish(UNITS - 1)

@@ -1,7 +1,7 @@
 import concourse.mybir as mybir
 from concourse.masks import make_identity
 
-F32, BF16, U16 = mybir.dt.float32, mybir.dt.bfloat16, mybir.dt.uint16
+F32, BF16, U16, I32 = mybir.dt.float32, mybir.dt.bfloat16, mybir.dt.uint16, mybir.dt.int32
 ACT = mybir.ActivationFunctionType
 ALU = mybir.AluOpType
 X_AXIS = mybir.AxisListType.X
@@ -12,12 +12,14 @@ UNITS = (B // P) * T
 KF = F // P
 KH = C1 // P
 BANK = 512
-FLIPS_IN_BANK = BANK // P
+PIECES = 2
+KP = KF // PIECES
 HZ = C1 + E
 WIDTH = C1 + C2
 W1_ROW = C1 + 16
 B1_ROW = C1 + 8
 H_COL, U_COL, Z_COL = 0, 1, 2
+LN2 = 0.6931471805599453
 
 FLOPS = 2 * B * T * (F * (E + C1 + C2) + C1 * C2)
 
@@ -27,7 +29,7 @@ def tile_forestclf_b_kernel(tc, d, wc, bc, w1, b1, w2, b2, offs, out):
     with (
         tc.tile_pool(name="held", bufs=1) as held,
         tc.tile_pool(name="windows", bufs=3) as windows,
-        tc.tile_pool(name="work", bufs=3) as work,
+        tc.tile_pool(name="work", bufs=4) as work,
         tc.psum_pool(name="psum_single", bufs=1) as psum_single,
         tc.psum_pool(name="psum_double", bufs=2) as psum_double,
     ):
@@ -43,51 +45,49 @@ def tile_forestclf_b_kernel(tc, d, wc, bc, w1, b1, w2, b2, offs, out):
         w1c = held.tile([P, T, KF, W1_ROW], BF16, name="w1c")
         b1c = held.tile([P, T, B1_ROW], F32, name="b1c")
         b2_all = held.tile([P, T, C2], F32, name="b2_all")
-        for t in range(T):
-            nc.scalar.dma_start(w1c[:, t, :, 0:C1], w1[t, :, :].rearrange("(a p) c -> p a c", p=P))
+        w2_rows = {}
+
+        def load_weights(t):
+            nc.sync.dma_start(w1c[:, t, :, 0:C1], w1[t, :, :].rearrange("(a p) c -> p a c", p=P))
             nc.scalar.dma_start(w1c[:, t, :, C1:HZ], wc[t, :, :].rearrange("(a p) e -> p a e", p=P))
             nc.scalar.dma_start(b1c[:, t, 0:C1], b1[t, :].partition_broadcast(P))
             nc.scalar.dma_start(b1c[:, t, C1:HZ], bc[t, :].partition_broadcast(P))
-        for t in range(T):
-            nc.scalar.dma_start(b2_all[:, t, :], b2[t, :].partition_broadcast(P))
-
-        w2_rows = {}
-
-        def load_w2(t):
             for a in range(KF + KH):
                 w2_rows[t, a] = held.tile([P, C2], BF16, name="w2_rows_%d_%d" % (t, a))
                 nc.sync.dma_start(w2_rows[t, a][:], w2[t, a * P : (a + 1) * P, :])
+            nc.sync.dma_start(b2_all[:, t, :], b2[t, :].partition_broadcast(P))
 
         load_window(0)
-        load_w2(0)
+        load_weights(0)
         load_window(1)
-        load_w2(1)
+        load_weights(1)
         load_window(2)
 
         ident_f32 = held.tile([P, P], F32, name="ident_f32")
         make_identity(nc, ident_f32[:])
         ident_bf16 = held.tile([P, P], BF16, name="ident_bf16")
-        make_identity(nc, ident_bf16[:])
+        nc.scalar.copy(ident_bf16[:], ident_f32[:])
 
         picked, flipped, h_bank, hz, relu, relu_bank, relu_flipped = {}, {}, {}, {}, {}, {}, {}
-        u_bank, u_biased, neg_max, exp_sum, log_sum = {}, {}, {}, {}, {}
+        u_bank, u_biased, neg_max, exp_sum, log_sum, inverse = {}, {}, {}, {}, {}, {}
 
         def gather(k):
             i, t = divmod(k, T)
-            picked[k] = work.tile([P, F], F32, name="picked")
-            piece = offsets[:, t * (F // 16) : (t + 1) * (F // 16)]
-            nc.scalar.activation(picked[k][:], window[i][:].indirect(piece), ACT.Copy)
+            for g in range(PIECES):
+                picked[k, g] = work.tile([P, KP * P], F32, name="picked_%d" % g)
+                first = (t * F + g * KP * P) // 16
+                piece = offsets[:, first : first + KP * P // 16]
+                nc.scalar.activation(picked[k, g][:], window[i][:].indirect(piece), ACT.Copy)
             if t == T - 1 and i + 3 < B // P:
                 load_window(i + 3)
 
         def flip(k):
             flipped[k] = work.tile([P, KF, P], BF16, name="flipped")
-            for first in range(0, KF, FLIPS_IN_BANK):
-                count = min(FLIPS_IN_BANK, KF - first)
-                bank = psum_single.tile([P, count, P], F32, name="flip_bank_%d" % first)
-                for a in range(count):
-                    nc.tensor.transpose(bank[:, a, :], picked[k][:, (first + a) * P : (first + a + 1) * P], ident_f32[:])
-                nc.scalar.copy(flipped[k][:, first : first + count, :], bank[:])
+            for g in range(PIECES):
+                bank = psum_single.tile([P, KP, P], F32, name="flip_bank_%d" % g)
+                for a in range(KP):
+                    nc.tensor.transpose(bank[:, a, :], picked[k, g][:, a * P : (a + 1) * P], ident_f32[:])
+                nc.scalar.copy(flipped[k][:, g * KP : (g + 1) * KP, :], bank[:])
 
         def hidden_product(k):
             t = k % T
@@ -142,10 +142,22 @@ def tile_forestclf_b_kernel(tc, d, wc, bc, w1, b1, w2, b2, offs, out):
                 cols = slice(n * BANK, (n + 1) * BANK)
                 nc.vector.tensor_tensor(u_biased[k][:, cols], u_bank[k, n][:], b2_all[:, t, cols], ALU.add)
 
-        def wide_softmax_sum(k):
-            softmax_sum(k, U_COL, u_biased[k][:])
+        def log_guess(k):
+            bits = work.tile([P, 3], F32, name="bits")
+            nc.vector.tensor_copy(bits[:], exp_sum[k][:].bitcast(I32))
             log_sum[k] = work.tile([P, 3], F32, name="log_sum")
-            nc.scalar.activation(log_sum[k][:], exp_sum[k][:], ACT.Ln)
+            nc.vector.tensor_scalar(log_sum[k][:], bits[:], LN2 / 2.0**23, -127.0 * LN2, ALU.mult, ALU.add)
+
+        def newton_exp(k):
+            inverse[k] = work.tile([P, 3], F32, name="inverse")
+            nc.scalar.activation(inverse[k][:], log_sum[k][:], ACT.Exp, scale=-1.0)
+
+        def newton_step(k):
+            ratio = work.tile([P, 3], F32, name="ratio")
+            nc.vector.tensor_tensor(ratio[:], inverse[k][:], exp_sum[k][:], ALU.mult)
+            better = work.tile([P, 3], F32, name="log_sum")
+            nc.vector.scalar_tensor_tensor(better[:], log_sum[k][:], -1.0, ratio[:], ALU.add, ALU.add)
+            log_sum[k] = better
 
         def finish(k):
             i, t = divmod(k, T)
@@ -162,33 +174,45 @@ def tile_forestclf_b_kernel(tc, d, wc, bc, w1, b1, w2, b2, offs, out):
             )
             nc.sync.dma_start(out[i * P : (i + 1) * P, t * WIDTH : (t + 1) * WIDTH], result[:])
 
+        def live(j):
+            return 0 <= j < UNITS
+
         gather(0)
         flip(0)
-        gather(1)
         hidden_product(0)
+        gather(1)
         flip(1)
         gather(2)
-        for k in range(UNITS):
-            for n in range(C2 // BANK):
-                u_bank[k, n] = psum_double.tile([P, BANK], F32, name="u_bank_%d" % n)
-            wide_product(k, range(0, KF // 2))
-            if k >= 1:
+        for k in range(UNITS + 2):
+            if live(k):
+                for n in range(C2 // BANK):
+                    u_bank[k, n] = psum_double.tile([P, BANK], F32, name="u_bank_%d" % n)
+                wide_product(k, range(0, KF // 2))
+            if live(k - 1):
                 wide_bias(k - 1)
-            hidden_bias(k)
-            flip_relu(k)
-            if k >= 1:
-                wide_softmax_sum(k - 1)
-            hidden_softmax_sums(k)
-            if k + 3 < UNITS:
+            if live(k):
+                hidden_bias(k)
+                flip_relu(k)
+            if live(k - 2):
+                log_guess(k - 2)
+                newton_exp(k - 2)
+            if live(k - 1):
+                softmax_sum(k - 1, U_COL, u_biased[k - 1][:])
+            if live(k - 2):
+                newton_step(k - 2)
+                newton_exp(k - 2)
+            if live(k):
+                hidden_softmax_sums(k)
+                copy_flipped_relu(k)
+            if live(k - 2):
+                newton_step(k - 2)
+            if live(k + 3):
                 gather(k + 3)
-            copy_flipped_relu(k)
-            wide_product(k, range(KF // 2, KF + KH))
-            if k >= 1:
-                finish(k - 1)
-            if k + 1 < UNITS:
+            if live(k):
+                wide_product(k, range(KF // 2, KF + KH))
+            if live(k - 2):
+                finish(k - 2)
+            if live(k + 1):
                 hidden_product(k + 1)
-            if k + 2 < UNITS:
+            if live(k + 2):
                 flip(k + 2)
-        wide_bias(UNITS - 1)
-        wide_softmax_sum(UNITS - 1)
-        finish(UNITS - 1)

@@ -47,29 +47,38 @@ def tile_forestclf_b_kernel(tc, d, wc, bc, w1, b1, w2, b2, offs, out):
         b2_all = held.tile([P, T, C2], F32, name="b2_all")
         w2_rows = {}
 
-        def load_weights(t):
+        def load_hidden_weights(t):
+            small_queue = nc.scalar if t == 0 else nc.gpsimd
+            small_queue.dma_start(w1c[:, t, :, C1:HZ], wc[t, :, :].rearrange("(a p) e -> p a e", p=P))
             nc.sync.dma_start(w1c[:, t, :, 0:C1], w1[t, :, :].rearrange("(a p) c -> p a c", p=P))
-            nc.scalar.dma_start(w1c[:, t, :, C1:HZ], wc[t, :, :].rearrange("(a p) e -> p a e", p=P))
-            nc.scalar.dma_start(b1c[:, t, 0:C1], b1[t, :].partition_broadcast(P))
-            nc.scalar.dma_start(b1c[:, t, C1:HZ], bc[t, :].partition_broadcast(P))
+            nc.sync.dma_start(b1c[:, t, 0:C1], b1[t, :].partition_broadcast(P))
+            nc.sync.dma_start(b1c[:, t, C1:HZ], bc[t, :].partition_broadcast(P))
+
+        def load_wide_weights(t):
             for a in range(KF + KH):
                 w2_rows[t, a] = held.tile([P, C2], BF16, name="w2_rows_%d_%d" % (t, a))
                 nc.sync.dma_start(w2_rows[t, a][:], w2[t, a * P : (a + 1) * P, :])
             nc.sync.dma_start(b2_all[:, t, :], b2[t, :].partition_broadcast(P))
 
-        load_window(0)
-        load_weights(0)
-        load_window(1)
-        load_weights(1)
-        load_window(2)
-
         ident_f32 = held.tile([P, P], F32, name="ident_f32")
         make_identity(nc, ident_f32[:])
-        ident_bf16 = held.tile([P, P], BF16, name="ident_bf16")
-        nc.scalar.copy(ident_bf16[:], ident_f32[:])
 
-        picked, flipped, h_bank, hz, relu, relu_bank, relu_flipped = {}, {}, {}, {}, {}, {}, {}
+        load_window(0)
+        load_hidden_weights(0)
+        load_window(1)
+        load_wide_weights(0)
+        load_hidden_weights(1)
+        load_wide_weights(1)
+        load_window(2)
+
+        ident_bf16 = held.tile([P, P], BF16, name="ident_bf16")
+        nc.scalar.activation(ident_bf16[:], ident_f32[:], ACT.Copy)
+
+        picked, rounded, flip_bank, flipped, h_bank, hz, relu, relu_bank, relu_flipped = {}, {}, {}, {}, {}, {}, {}, {}, {}
         u_bank, u_biased, neg_max, exp_sum, log_sum, inverse = {}, {}, {}, {}, {}, {}
+
+        def live(j):
+            return 0 <= j < UNITS
 
         def gather(k):
             i, t = divmod(k, T)
@@ -78,16 +87,23 @@ def tile_forestclf_b_kernel(tc, d, wc, bc, w1, b1, w2, b2, offs, out):
                 first = (t * F + g * KP * P) // 16
                 piece = offsets[:, first : first + KP * P // 16]
                 nc.scalar.activation(picked[k, g][:], window[i][:].indirect(piece), ACT.Copy)
+                rounded[k, g] = work.tile([P, KP * P], BF16, name="rounded_%d" % g)
+                nc.vector.tensor_copy(rounded[k, g][:], picked[k, g][:])
             if t == T - 1 and i + 3 < B // P:
                 load_window(i + 3)
 
+        def flip_block(k, a):
+            if a == 0:
+                flip_bank[k] = psum_double.tile([P, KF, P], BF16, name="flip_bank")
+            g, a_in_piece = divmod(a, KP)
+            nc.tensor.transpose(flip_bank[k][:, a, :], rounded[k, g][:, a_in_piece * P : (a_in_piece + 1) * P], ident_bf16[:])
+            if a == KF - 1:
+                flipped[k] = work.tile([P, KF, P], BF16, name="flipped")
+                nc.scalar.copy(flipped[k][:], flip_bank[k][:])
+
         def flip(k):
-            flipped[k] = work.tile([P, KF, P], BF16, name="flipped")
-            for g in range(PIECES):
-                bank = psum_single.tile([P, KP, P], F32, name="flip_bank_%d" % g)
-                for a in range(KP):
-                    nc.tensor.transpose(bank[:, a, :], picked[k, g][:, a * P : (a + 1) * P], ident_f32[:])
-                nc.scalar.copy(flipped[k][:, g * KP : (g + 1) * KP, :], bank[:])
+            for a in range(KF):
+                flip_block(k, a)
 
         def hidden_product(k):
             t = k % T
@@ -120,6 +136,8 @@ def tile_forestclf_b_kernel(tc, d, wc, bc, w1, b1, w2, b2, offs, out):
                         u_bank[k, n][:], lhsT=stationary, rhs=w2_rows[t, a][:, n * BANK : (n + 1) * BANK],
                         start=(a == 0), stop=(a == KF + KH - 1),
                     )
+                if a < KF and live(k + 2):
+                    flip_block(k + 2, a)
 
         def softmax_sum(k, col, values):
             nc.vector.tensor_reduce(neg_max[k][:, col : col + 1], values, X_AXIS, ALU.max, negate=True)
@@ -174,15 +192,13 @@ def tile_forestclf_b_kernel(tc, d, wc, bc, w1, b1, w2, b2, offs, out):
             )
             nc.sync.dma_start(out[i * P : (i + 1) * P, t * WIDTH : (t + 1) * WIDTH], result[:])
 
-        def live(j):
-            return 0 <= j < UNITS
-
         gather(0)
         flip(0)
         hidden_product(0)
         gather(1)
         flip(1)
         gather(2)
+        gather(3)
         for k in range(UNITS + 2):
             if live(k):
                 for n in range(C2 // BANK):
@@ -206,13 +222,11 @@ def tile_forestclf_b_kernel(tc, d, wc, bc, w1, b1, w2, b2, offs, out):
                 copy_flipped_relu(k)
             if live(k - 2):
                 newton_step(k - 2)
-            if live(k + 3):
-                gather(k + 3)
+            if live(k + 4):
+                gather(k + 4)
             if live(k):
                 wide_product(k, range(KF // 2, KF + KH))
             if live(k - 2):
                 finish(k - 2)
             if live(k + 1):
                 hidden_product(k + 1)
-            if live(k + 2):
-                flip(k + 2)

@@ -12,8 +12,6 @@ UNITS = (B // P) * T
 KF = F // P
 KH = C1 // P
 BANK = 512
-PIECES = 2
-KP = KF // PIECES
 HZ = C1 + E
 WIDTH = C1 + C2
 W1_ROW = C1 + 16
@@ -48,20 +46,23 @@ def tile_forestclf_b_kernel(tc, d, wc, bc, w1, b1, w2, b2, offs, out):
         w2_rows = {}
 
         def load_hidden_weights(t):
-            small_queue = nc.scalar if t == 0 else nc.gpsimd
-            small_queue.dma_start(w1c[:, t, :, C1:HZ], wc[t, :, :].rearrange("(a p) e -> p a e", p=P))
-            nc.sync.dma_start(w1c[:, t, :, 0:C1], w1[t, :, :].rearrange("(a p) c -> p a c", p=P))
+            nc.sync.dma_start(w1c[:, t, :, 0:C1], w1[t, :, :].rearrange("(p a) c -> p a c", a=KF))
             nc.sync.dma_start(b1c[:, t, 0:C1], b1[t, :].partition_broadcast(P))
             nc.sync.dma_start(b1c[:, t, C1:HZ], bc[t, :].partition_broadcast(P))
 
         def load_wide_weights(t):
+            feature_rows = w2[t, 0:F, :].rearrange("(p a) k -> a p k", a=KF)
             for a in range(KF + KH):
                 w2_rows[t, a] = held.tile([P, C2], BF16, name="w2_rows_%d_%d" % (t, a))
-                nc.sync.dma_start(w2_rows[t, a][:], w2[t, a * P : (a + 1) * P, :])
+                nc.sync.dma_start(w2_rows[t, a][:], feature_rows[a, :, :] if a < KF else w2[t, a * P : (a + 1) * P, :])
             nc.sync.dma_start(b2_all[:, t, :], b2[t, :].partition_broadcast(P))
 
-        ident_f32 = held.tile([P, P], F32, name="ident_f32")
-        make_identity(nc, ident_f32[:])
+        identity = held.tile([P, P], BF16, name="identity")
+        make_identity(nc, identity[:])
+
+        wc_dense = held.tile([P, T, KF, E], BF16, name="wc_dense")
+        nc.sync.dma_start(wc_dense[:], wc.rearrange("t (p a) e -> p t a e", a=KF))
+        nc.vector.tensor_copy(w1c[:, :, :, C1:HZ], wc_dense[:])
 
         load_window(0)
         load_hidden_weights(0)
@@ -71,10 +72,7 @@ def tile_forestclf_b_kernel(tc, d, wc, bc, w1, b1, w2, b2, offs, out):
         load_wide_weights(1)
         load_window(2)
 
-        ident_bf16 = held.tile([P, P], BF16, name="ident_bf16")
-        nc.scalar.activation(ident_bf16[:], ident_f32[:], ACT.Copy)
-
-        picked, rounded, flip_bank, flipped, h_bank, hz, relu, relu_bank, relu_flipped = {}, {}, {}, {}, {}, {}, {}, {}, {}
+        rounded, flip_bank, flipped, h_bank, hz, relu, relu_bank, relu_flipped = {}, {}, {}, {}, {}, {}, {}, {}
         u_bank, u_biased, neg_max, exp_sum, log_sum, inverse = {}, {}, {}, {}, {}, {}
 
         def live(j):
@@ -82,21 +80,18 @@ def tile_forestclf_b_kernel(tc, d, wc, bc, w1, b1, w2, b2, offs, out):
 
         def gather(k):
             i, t = divmod(k, T)
-            for g in range(PIECES):
-                picked[k, g] = work.tile([P, KP * P], F32, name="picked_%d" % g)
-                first = (t * F + g * KP * P) // 16
-                piece = offsets[:, first : first + KP * P // 16]
-                nc.scalar.activation(picked[k, g][:], window[i][:].indirect(piece), ACT.Copy)
-                rounded[k, g] = work.tile([P, KP * P], BF16, name="rounded_%d" % g)
-                nc.vector.tensor_copy(rounded[k, g][:], picked[k, g][:])
+            picked = work.tile([P, F], F32, name="picked")
+            piece = offsets[:, t * (F // 16) : (t + 1) * (F // 16)]
+            nc.scalar.activation(picked[:], window[i][:].indirect(piece), ACT.Copy)
+            rounded[k] = work.tile([P, F], BF16, name="rounded")
+            nc.vector.tensor_copy(rounded[k][:], picked[:])
             if t == T - 1 and i + 3 < B // P:
                 load_window(i + 3)
 
         def flip_block(k, a):
             if a == 0:
                 flip_bank[k] = psum_double.tile([P, KF, P], BF16, name="flip_bank")
-            g, a_in_piece = divmod(a, KP)
-            nc.tensor.transpose(flip_bank[k][:, a, :], rounded[k, g][:, a_in_piece * P : (a_in_piece + 1) * P], ident_bf16[:])
+            nc.tensor.transpose(flip_bank[k][:, a, :], rounded[k][:, a:F:KF], identity[:])
             if a == KF - 1:
                 flipped[k] = work.tile([P, KF, P], BF16, name="flipped")
                 nc.scalar.copy(flipped[k][:], flip_bank[k][:])
@@ -121,7 +116,7 @@ def tile_forestclf_b_kernel(tc, d, wc, bc, w1, b1, w2, b2, offs, out):
         def flip_relu(k):
             relu_bank[k] = psum_single.tile([P, KH, P], BF16, name="relu_bank")
             for a in range(KH):
-                nc.tensor.transpose(relu_bank[k][:, a, :], relu[k][:, a * P : (a + 1) * P], ident_bf16[:])
+                nc.tensor.transpose(relu_bank[k][:, a, :], relu[k][:, a * P : (a + 1) * P], identity[:])
 
         def copy_flipped_relu(k):
             relu_flipped[k] = work.tile([P, KH, P], BF16, name="relu_flipped")
@@ -161,10 +156,8 @@ def tile_forestclf_b_kernel(tc, d, wc, bc, w1, b1, w2, b2, offs, out):
                 nc.vector.tensor_tensor(u_biased[k][:, cols], u_bank[k, n][:], b2_all[:, t, cols], ALU.add)
 
         def log_guess(k):
-            bits = work.tile([P, 3], F32, name="bits")
-            nc.vector.tensor_copy(bits[:], exp_sum[k][:].bitcast(I32))
             log_sum[k] = work.tile([P, 3], F32, name="log_sum")
-            nc.vector.tensor_scalar(log_sum[k][:], bits[:], LN2 / 2.0**23, -127.0 * LN2, ALU.mult, ALU.add)
+            nc.vector.tensor_scalar(log_sum[k][:], exp_sum[k][:].bitcast(I32), LN2 / 2.0**23, -127.0 * LN2, ALU.mult, ALU.add)
 
         def newton_exp(k):
             inverse[k] = work.tile([P, 3], F32, name="inverse")

@@ -12,6 +12,7 @@ UNITS = (B // P) * T
 KF = F // P
 KH = C1 // P
 BANK = 512
+WINDOWS = 3
 HZ = C1 + E
 WIDTH = C1 + C2
 W1_ROW = C1 + 16
@@ -26,7 +27,7 @@ def tile_forestclf_b_kernel(tc, d, wc, bc, w1, b1, w2, b2, offs, out):
     nc = tc.nc
     with (
         tc.tile_pool(name="held", bufs=1) as held,
-        tc.tile_pool(name="windows", bufs=3) as windows,
+        tc.tile_pool(name="windows", bufs=WINDOWS) as windows,
         tc.tile_pool(name="work", bufs=4) as work,
         tc.psum_pool(name="psum_single", bufs=1) as psum_single,
         tc.psum_pool(name="psum_double", bufs=2) as psum_double,
@@ -85,8 +86,8 @@ def tile_forestclf_b_kernel(tc, d, wc, bc, w1, b1, w2, b2, offs, out):
             nc.scalar.activation(picked[:], window[i][:].indirect(piece), ACT.Copy)
             rounded[k] = work.tile([P, F], BF16, name="rounded")
             nc.vector.tensor_copy(rounded[k][:], picked[:])
-            if t == T - 1 and i + 3 < B // P:
-                load_window(i + 3)
+            if t == T - 1 and i + WINDOWS < B // P:
+                load_window(i + WINDOWS)
 
         def flip_block(k, a):
             if a == 0:
@@ -207,12 +208,13 @@ def tile_forestclf_b_kernel(tc, d, wc, bc, w1, b1, w2, b2, offs, out):
                 newton_exp(k - 2)
             if live(k - 1):
                 softmax_sum(k - 1, U_COL, u_biased[k - 1][:])
+            if live(k):
+                copy_flipped_relu(k)
             if live(k - 2):
                 newton_step(k - 2)
                 newton_exp(k - 2)
             if live(k):
                 hidden_softmax_sums(k)
-                copy_flipped_relu(k)
             if live(k - 2):
                 newton_step(k - 2)
             if live(k + 4):

@@ -32,6 +32,11 @@ def tile_forestclf_b_kernel(tc, d, wc, bc, w1, b1, w2, b2, offs, out):
         tc.psum_pool(name="psum_single", bufs=1) as psum_single,
         tc.psum_pool(name="psum_double", bufs=2) as psum_double,
     ):
+        zero = held.tile([P, 1], F32, name="zero")
+        nc.vector.memset(zero[:], 0.0)
+        one = held.tile([P, 1], F32, name="one")
+        nc.scalar.activation(one[:], zero[:], ACT.Exp)
+
         offsets = held.tile([P, T * F // 16], U16, name="offsets")
         nc.sync.dma_start(offsets[:], offs)
 
@@ -51,11 +56,13 @@ def tile_forestclf_b_kernel(tc, d, wc, bc, w1, b1, w2, b2, offs, out):
             nc.sync.dma_start(b1c[:, t, 0:C1], b1[t, :].partition_broadcast(P))
             nc.sync.dma_start(b1c[:, t, C1:HZ], bc[t, :].partition_broadcast(P))
 
-        def load_wide_weights(t):
+        def load_wide_weights(t, row_blocks):
             feature_rows = w2[t, 0:F, :].rearrange("(p a) k -> a p k", a=KF)
-            for a in range(KF + KH):
+            for a in row_blocks:
                 w2_rows[t, a] = held.tile([P, C2], BF16, name="w2_rows_%d_%d" % (t, a))
                 nc.sync.dma_start(w2_rows[t, a][:], feature_rows[a, :, :] if a < KF else w2[t, a * P : (a + 1) * P, :])
+
+        def load_wide_bias(t):
             nc.sync.dma_start(b2_all[:, t, :], b2[t, :].partition_broadcast(P))
 
         identity = held.tile([P, P], BF16, name="identity")
@@ -67,20 +74,28 @@ def tile_forestclf_b_kernel(tc, d, wc, bc, w1, b1, w2, b2, offs, out):
 
         load_window(0)
         load_hidden_weights(0)
+        load_wide_weights(0, range(0, 4))
         load_window(1)
-        load_wide_weights(0)
-        load_hidden_weights(1)
-        load_wide_weights(1)
+        load_wide_weights(0, range(4, KF + KH))
+        load_wide_bias(0)
         load_window(2)
+        load_hidden_weights(1)
+        load_wide_weights(1, range(0, KF + KH))
+        load_wide_bias(1)
 
         rounded, flip_bank, flipped, h_bank, hz, relu, relu_bank, relu_flipped = {}, {}, {}, {}, {}, {}, {}, {}
-        u_bank, u_biased, neg_max, exp_sum, log_sum, inverse = {}, {}, {}, {}, {}, {}
+        u_bank, u_biased, neg_max, exp_sum, inverse, log_base = {}, {}, {}, {}, {}, {}
 
         def live(j):
             return 0 <= j < UNITS
 
+        def block_and_tree(k):
+            group, rest = divmod(k, 2 * T)
+            t, j = divmod(rest, 2)
+            return 2 * group + j, t
+
         def gather(k):
-            i, t = divmod(k, T)
+            i, t = block_and_tree(k)
             picked = work.tile([P, F], F32, name="picked")
             piece = offsets[:, t * (F // 16) : (t + 1) * (F // 16)]
             nc.scalar.activation(picked[:], window[i][:].indirect(piece), ACT.Copy)
@@ -102,13 +117,13 @@ def tile_forestclf_b_kernel(tc, d, wc, bc, w1, b1, w2, b2, offs, out):
                 flip_block(k, a)
 
         def hidden_product(k):
-            t = k % T
+            t = block_and_tree(k)[1]
             h_bank[k] = psum_single.tile([P, HZ], F32, name="h_bank")
             for a in range(KF):
                 nc.tensor.matmul(h_bank[k][:], lhsT=flipped[k][:, a, :], rhs=w1c[:, t, a, 0:HZ], start=(a == 0), stop=(a == KF - 1))
 
         def hidden_bias(k):
-            t = k % T
+            t = block_and_tree(k)[1]
             hz[k] = work.tile([P, HZ], F32, name="hz")
             nc.vector.tensor_tensor(hz[k][:], h_bank[k][:], b1c[:, t, 0:HZ], ALU.add)
             relu[k] = work.tile([P, C1], BF16, name="relu")
@@ -124,7 +139,7 @@ def tile_forestclf_b_kernel(tc, d, wc, bc, w1, b1, w2, b2, offs, out):
             nc.vector.tensor_copy(relu_flipped[k][:], relu_bank[k][:])
 
         def wide_product(k, row_blocks):
-            t = k % T
+            t = block_and_tree(k)[1]
             for a in row_blocks:
                 stationary = flipped[k][:, a, :] if a < KF else relu_flipped[k][:, a - KF, :]
                 for n in range(C2 // BANK):
@@ -150,31 +165,32 @@ def tile_forestclf_b_kernel(tc, d, wc, bc, w1, b1, w2, b2, offs, out):
             softmax_sum(k, Z_COL, hz[k][:, C1:HZ])
 
         def wide_bias(k):
-            t = k % T
+            t = block_and_tree(k)[1]
             u_biased[k] = work.tile([P, C2], F32, name="u_biased")
             for n in range(C2 // BANK):
                 cols = slice(n * BANK, (n + 1) * BANK)
                 nc.vector.tensor_tensor(u_biased[k][:, cols], u_bank[k, n][:], b2_all[:, t, cols], ALU.add)
 
         def log_guess(k):
-            log_sum[k] = work.tile([P, 3], F32, name="log_sum")
-            nc.vector.tensor_scalar(log_sum[k][:], exp_sum[k][:].bitcast(I32), LN2 / 2.0**23, -127.0 * LN2, ALU.mult, ALU.add)
-
-        def newton_exp(k):
+            guess = work.tile([P, 3], F32, name="guess")
+            nc.vector.tensor_scalar(
+                guess[:], exp_sum[k][:].bitcast(I32), LN2 / 2.0**23, (0.0861 / 2.0 - 127.0) * LN2, ALU.mult, ALU.add
+            )
             inverse[k] = work.tile([P, 3], F32, name="inverse")
-            nc.scalar.activation(inverse[k][:], log_sum[k][:], ACT.Exp, scale=-1.0)
-
-        def newton_step(k):
-            ratio = work.tile([P, 3], F32, name="ratio")
-            nc.vector.tensor_tensor(ratio[:], inverse[k][:], exp_sum[k][:], ALU.mult)
-            better = work.tile([P, 3], F32, name="log_sum")
-            nc.vector.scalar_tensor_tensor(better[:], log_sum[k][:], -1.0, ratio[:], ALU.add, ALU.add)
-            log_sum[k] = better
+            nc.scalar.activation(inverse[k][:], guess[:], ACT.Exp, scale=-1.0)
+            log_base[k] = work.tile([P, 3], F32, name="log_base")
+            nc.vector.scalar_tensor_tensor(log_base[k][:], guess[:], -1.5, neg_max[k][:], ALU.add, ALU.subtract)
 
         def finish(k):
-            i, t = divmod(k, T)
+            i, t = block_and_tree(k)
+            ratio = work.tile([P, 3], F32, name="ratio")
+            nc.vector.tensor_tensor(ratio[:], inverse[k][:], exp_sum[k][:], ALU.mult)
+            bracket = work.tile([P, 3], F32, name="bracket")
+            nc.vector.tensor_scalar(bracket[:], ratio[:], -0.5, 2.0, ALU.mult, ALU.add)
+            series = work.tile([P, 3], F32, name="series")
+            nc.vector.tensor_tensor(series[:], ratio[:], bracket[:], ALU.mult)
             log_norm = work.tile([P, 3], F32, name="log_norm")
-            nc.vector.tensor_tensor(log_norm[:], log_sum[k][:], neg_max[k][:], ALU.subtract)
+            nc.vector.tensor_tensor(log_norm[:], series[:], log_base[k][:], ALU.add)
             neg_lw = work.tile([P, 1], F32, name="neg_lw")
             nc.vector.tensor_tensor(neg_lw[:], log_norm[:, Z_COL : Z_COL + 1], hz[k][:, C1 + 1 : C1 + 2], ALU.subtract)
             result = work.tile([P, WIDTH], F32, name="result")
@@ -189,9 +205,9 @@ def tile_forestclf_b_kernel(tc, d, wc, bc, w1, b1, w2, b2, offs, out):
         gather(0)
         flip(0)
         hidden_product(0)
+        gather(2)
         gather(1)
         flip(1)
-        gather(2)
         gather(3)
         for k in range(UNITS + 2):
             if live(k):
@@ -205,18 +221,12 @@ def tile_forestclf_b_kernel(tc, d, wc, bc, w1, b1, w2, b2, offs, out):
                 flip_relu(k)
             if live(k - 2):
                 log_guess(k - 2)
-                newton_exp(k - 2)
             if live(k - 1):
                 softmax_sum(k - 1, U_COL, u_biased[k - 1][:])
             if live(k):
                 copy_flipped_relu(k)
-            if live(k - 2):
-                newton_step(k - 2)
-                newton_exp(k - 2)
             if live(k):
                 hidden_softmax_sums(k)
-            if live(k - 2):
-                newton_step(k - 2)
             if live(k + 4):
                 gather(k + 4)
             if live(k):

@@ -58,14 +58,15 @@ def tile_forestclf_b_kernel(tc, d, wc, bc, w1, b1, w2, b2, offs, out):
 
         def load_wide_weights(t, row_blocks):
             feature_rows = w2[t, 0:F, :].rearrange("(p a) k -> a p k", a=KF)
+            hidden_rows = w2[t, F : F + C1, :].rearrange("(p a) k -> a p k", a=KH)
             for a in row_blocks:
                 w2_rows[t, a] = held.tile([P, C2], BF16, name="w2_rows_%d_%d" % (t, a))
-                nc.sync.dma_start(w2_rows[t, a][:], feature_rows[a, :, :] if a < KF else w2[t, a * P : (a + 1) * P, :])
+                nc.sync.dma_start(w2_rows[t, a][:], feature_rows[a, :, :] if a < KF else hidden_rows[a - KF, :, :])
 
         def load_wide_bias(t):
             nc.sync.dma_start(b2_all[:, t, :], b2[t, :].partition_broadcast(P))
 
-        identity = held.tile([P, P], BF16, name="identity")
+        identity = held.tile([P, P], F32, name="identity")
         make_identity(nc, identity[:])
 
         wc_dense = held.tile([P, T, KF, E], BF16, name="wc_dense")
@@ -74,9 +75,8 @@ def tile_forestclf_b_kernel(tc, d, wc, bc, w1, b1, w2, b2, offs, out):
 
         load_window(0)
         load_hidden_weights(0)
-        load_wide_weights(0, range(0, 4))
         load_window(1)
-        load_wide_weights(0, range(4, KF + KH))
+        load_wide_weights(0, range(0, KF + KH))
         load_wide_bias(0)
         load_window(2)
         load_hidden_weights(1)
@@ -104,23 +104,26 @@ def tile_forestclf_b_kernel(tc, d, wc, bc, w1, b1, w2, b2, offs, out):
             if t == T - 1 and i + WINDOWS < B // P:
                 load_window(i + WINDOWS)
 
-        def flip_block(k, a):
-            if a == 0:
-                flip_bank[k] = psum_double.tile([P, KF, P], BF16, name="flip_bank")
-            nc.tensor.transpose(flip_bank[k][:, a, :], rounded[k][:, a:F:KF], identity[:])
-            if a == KF - 1:
-                flipped[k] = work.tile([P, KF, P], BF16, name="flipped")
-                nc.scalar.copy(flipped[k][:], flip_bank[k][:])
+        def flip_block(k, g):
+            if g == 0:
+                flip_bank[k] = psum_double.tile([P, KF // 2, P], F32, name="flip_bank")
+            nc.tensor.transpose(flip_bank[k][:, g, :], rounded[k][:].bitcast(F32)[:, g : F // 2 : KF // 2], identity[:])
+            if g == KF // 2 - 1:
+                flipped[k] = work.tile([P, KF // 2, 2 * P], BF16, name="flipped")
+                nc.scalar.copy(flipped[k][:], flip_bank[k][:].bitcast(BF16))
 
         def flip(k):
-            for a in range(KF):
-                flip_block(k, a)
+            for g in range(KF // 2):
+                flip_block(k, g)
+
+        def feature_block(k, a):
+            return flipped[k][:, a // 2, a % 2 : 2 * P : 2]
 
         def hidden_product(k):
             t = block_and_tree(k)[1]
             h_bank[k] = psum_single.tile([P, HZ], F32, name="h_bank")
             for a in range(KF):
-                nc.tensor.matmul(h_bank[k][:], lhsT=flipped[k][:, a, :], rhs=w1c[:, t, a, 0:HZ], start=(a == 0), stop=(a == KF - 1))
+                nc.tensor.matmul(h_bank[k][:], lhsT=feature_block(k, a), rhs=w1c[:, t, a, 0:HZ], start=(a == 0), stop=(a == KF - 1))
 
         def hidden_bias(k):
             t = block_and_tree(k)[1]
@@ -130,25 +133,24 @@ def tile_forestclf_b_kernel(tc, d, wc, bc, w1, b1, w2, b2, offs, out):
             nc.vector.tensor_scalar_max(relu[k][:], hz[k][:, 0:C1], 0.0)
 
         def flip_relu(k):
-            relu_bank[k] = psum_single.tile([P, KH, P], BF16, name="relu_bank")
-            for a in range(KH):
-                nc.tensor.transpose(relu_bank[k][:, a, :], relu[k][:, a * P : (a + 1) * P], identity[:])
+            relu_bank[k] = psum_single.tile([P, P], F32, name="relu_bank")
+            nc.tensor.transpose(relu_bank[k][:], relu[k][:].bitcast(F32), identity[:])
 
         def copy_flipped_relu(k):
-            relu_flipped[k] = work.tile([P, KH, P], BF16, name="relu_flipped")
-            nc.vector.tensor_copy(relu_flipped[k][:], relu_bank[k][:])
+            relu_flipped[k] = work.tile([P, KH * P], BF16, name="relu_flipped")
+            nc.vector.tensor_copy(relu_flipped[k][:], relu_bank[k][:].bitcast(BF16))
 
         def wide_product(k, row_blocks):
             t = block_and_tree(k)[1]
             for a in row_blocks:
-                stationary = flipped[k][:, a, :] if a < KF else relu_flipped[k][:, a - KF, :]
+                stationary = feature_block(k, a) if a < KF else relu_flipped[k][:, a - KF : KH * P : KH]
                 for n in range(C2 // BANK):
                     nc.tensor.matmul(
                         u_bank[k, n][:], lhsT=stationary, rhs=w2_rows[t, a][:, n * BANK : (n + 1) * BANK],
                         start=(a == 0), stop=(a == KF + KH - 1),
                     )
-                if a < KF and live(k + 2):
-                    flip_block(k + 2, a)
+                if a % 2 == 0 and a < KF and live(k + 2):
+                    flip_block(k + 2, a // 2)
 
         def softmax_sum(k, col, values):
             nc.vector.tensor_reduce(neg_max[k][:, col : col + 1], values, X_AXIS, ALU.max, negate=True)
@@ -180,6 +182,8 @@ def tile_forestclf_b_kernel(tc, d, wc, bc, w1, b1, w2, b2, offs, out):
             nc.scalar.activation(inverse[k][:], guess[:], ACT.Exp, scale=-1.0)
             log_base[k] = work.tile([P, 3], F32, name="log_base")
             nc.vector.scalar_tensor_tensor(log_base[k][:], guess[:], -1.5, neg_max[k][:], ALU.add, ALU.subtract)
+            z_base = log_base[k][:, Z_COL : Z_COL + 1]
+            nc.vector.tensor_tensor(z_base, z_base, hz[k][:, C1 + 1 : C1 + 2], ALU.subtract)
 
         def finish(k):
             i, t = block_and_tree(k)
@@ -191,20 +195,20 @@ def tile_forestclf_b_kernel(tc, d, wc, bc, w1, b1, w2, b2, offs, out):
             nc.vector.tensor_tensor(series[:], ratio[:], bracket[:], ALU.mult)
             log_norm = work.tile([P, 3], F32, name="log_norm")
             nc.vector.tensor_tensor(log_norm[:], series[:], log_base[k][:], ALU.add)
-            neg_lw = work.tile([P, 1], F32, name="neg_lw")
-            nc.vector.tensor_tensor(neg_lw[:], log_norm[:, Z_COL : Z_COL + 1], hz[k][:, C1 + 1 : C1 + 2], ALU.subtract)
+            neg_lw = log_norm[:, Z_COL : Z_COL + 1]
             result = work.tile([P, WIDTH], F32, name="result")
             nc.vector.tensor_scalar(
-                result[:, 0:C1], hz[k][:, 0:C1], log_norm[:, H_COL : H_COL + 1], neg_lw[:], ALU.subtract, ALU.subtract
+                result[:, 0:C1], hz[k][:, 0:C1], log_norm[:, H_COL : H_COL + 1], neg_lw, ALU.subtract, ALU.subtract
             )
             nc.vector.tensor_scalar(
-                result[:, C1:WIDTH], u_biased[k][:], log_norm[:, U_COL : U_COL + 1], neg_lw[:], ALU.subtract, ALU.subtract
+                result[:, C1:WIDTH], u_biased[k][:], log_norm[:, U_COL : U_COL + 1], neg_lw, ALU.subtract, ALU.subtract
             )
             nc.sync.dma_start(out[i * P : (i + 1) * P, t * WIDTH : (t + 1) * WIDTH], result[:])
 
         gather(0)
         flip(0)
         hidden_product(0)
+        hidden_bias(0)
         gather(2)
         gather(1)
         flip(1)
@@ -214,24 +218,23 @@ def tile_forestclf_b_kernel(tc, d, wc, bc, w1, b1, w2, b2, offs, out):
                 for n in range(C2 // BANK):
                     u_bank[k, n] = psum_double.tile([P, BANK], F32, name="u_bank_%d" % n)
                 wide_product(k, range(0, KF // 2))
+                flip_relu(k)
+                copy_flipped_relu(k)
+                wide_product(k, range(KF // 2, KF))
+            if live(k + 1):
+                hidden_product(k + 1)
+                hidden_bias(k + 1)
+            if live(k):
+                wide_product(k, range(KF, KF + KH))
             if live(k - 1):
                 wide_bias(k - 1)
-            if live(k):
-                hidden_bias(k)
-                flip_relu(k)
             if live(k - 2):
                 log_guess(k - 2)
             if live(k - 1):
                 softmax_sum(k - 1, U_COL, u_biased[k - 1][:])
             if live(k):
-                copy_flipped_relu(k)
-            if live(k):
                 hidden_softmax_sums(k)
             if live(k + 4):
                 gather(k + 4)
-            if live(k):
-                wide_product(k, range(KF // 2, KF + KH))
             if live(k - 2):
                 finish(k - 2)
-            if live(k + 1):
-                hidden_product(k + 1)

@@ -1,7 +1,7 @@
 import concourse.mybir as mybir
 from concourse.masks import make_identity
 
-F32, BF16, U16, I32 = mybir.dt.float32, mybir.dt.bfloat16, mybir.dt.uint16, mybir.dt.int32
+F32, BF16, U16, I32, U32 = mybir.dt.float32, mybir.dt.bfloat16, mybir.dt.uint16, mybir.dt.int32, mybir.dt.uint32
 ACT = mybir.ActivationFunctionType
 ALU = mybir.AluOpType
 X_AXIS = mybir.AxisListType.X
@@ -19,6 +19,7 @@ W1_ROW = C1 + 16
 B1_ROW = C1 + 8
 H_COL, U_COL, Z_COL = 0, 1, 2
 LN2 = 0.6931471805599453
+GUESS_SCALE, GUESS_SHIFT = LN2 / 2.0**23, (0.0861 / 2.0 - 127.0) * LN2
 
 FLOPS = 2 * B * T * (F * (E + C1 + C2) + C1 * C2)
 
@@ -174,12 +175,10 @@ def tile_forestclf_b_kernel(tc, d, wc, bc, w1, b1, w2, b2, offs, out):
                 nc.vector.tensor_tensor(u_biased[k][:, cols], u_bank[k, n][:], b2_all[:, t, cols], ALU.add)
 
         def log_guess(k):
-            guess = work.tile([P, 3], F32, name="guess")
-            nc.vector.tensor_scalar(
-                guess[:], exp_sum[k][:].bitcast(I32), LN2 / 2.0**23, (0.0861 / 2.0 - 127.0) * LN2, ALU.mult, ALU.add
-            )
             inverse[k] = work.tile([P, 3], F32, name="inverse")
-            nc.scalar.activation(inverse[k][:], guess[:], ACT.Exp, scale=-1.0)
+            nc.scalar.activation(inverse[k][:], exp_sum[k][:].bitcast(U32), ACT.Exp, scale=-GUESS_SCALE, bias=-GUESS_SHIFT)
+            guess = work.tile([P, 3], F32, name="guess")
+            nc.vector.tensor_scalar(guess[:], exp_sum[k][:].bitcast(I32), GUESS_SCALE, GUESS_SHIFT, ALU.mult, ALU.add)
             log_base[k] = work.tile([P, 3], F32, name="log_base")
             nc.vector.scalar_tensor_tensor(log_base[k][:], guess[:], -1.5, neg_max[k][:], ALU.add, ALU.subtract)
             z_base = log_base[k][:, Z_COL : Z_COL + 1]

@@ -186,23 +186,23 @@ def tile_forestclf_b_kernel(tc, d, wc, bc, w1, b1, w2, b2, offs, out):
 
         def finish(k):
             i, t = block_and_tree(k)
-            ratio = work.tile([P, 3], F32, name="ratio")
-            nc.vector.tensor_tensor(ratio[:], inverse[k][:], exp_sum[k][:], ALU.mult)
-            bracket = work.tile([P, 3], F32, name="bracket")
-            nc.vector.tensor_scalar(bracket[:], ratio[:], -0.5, 2.0, ALU.mult, ALU.add)
-            series = work.tile([P, 3], F32, name="series")
-            nc.vector.tensor_tensor(series[:], ratio[:], bracket[:], ALU.mult)
+            neg_half = work.tile([P, 3], F32, name="neg_half")
+            nc.vector.scalar_tensor_tensor(neg_half[:], inverse[k][:], -0.5, exp_sum[k][:], ALU.mult, ALU.mult)
+            product = work.tile([P, 3], F32, name="product")
+            nc.vector.scalar_tensor_tensor(product[:], neg_half[:], 2.0, neg_half[:], ALU.add, ALU.mult)
             log_norm = work.tile([P, 3], F32, name="log_norm")
-            nc.vector.tensor_tensor(log_norm[:], series[:], log_base[k][:], ALU.add)
+            nc.vector.scalar_tensor_tensor(log_norm[:], product[:], -2.0, log_base[k][:], ALU.mult, ALU.add)
             neg_lw = log_norm[:, Z_COL : Z_COL + 1]
             result = work.tile([P, WIDTH], F32, name="result")
-            nc.vector.tensor_scalar(
-                result[:, 0:C1], hz[k][:, 0:C1], log_norm[:, H_COL : H_COL + 1], neg_lw, ALU.subtract, ALU.subtract
-            )
+            stored = out[i * P : (i + 1) * P, t * WIDTH : (t + 1) * WIDTH]
             nc.vector.tensor_scalar(
                 result[:, C1:WIDTH], u_biased[k][:], log_norm[:, U_COL : U_COL + 1], neg_lw, ALU.subtract, ALU.subtract
             )
-            nc.sync.dma_start(out[i * P : (i + 1) * P, t * WIDTH : (t + 1) * WIDTH], result[:])
+            nc.sync.dma_start(stored[:, C1:WIDTH], result[:, C1:WIDTH])
+            nc.vector.tensor_scalar(
+                result[:, 0:C1], hz[k][:, 0:C1], log_norm[:, H_COL : H_COL + 1], neg_lw, ALU.subtract, ALU.subtract
+            )
+            nc.sync.dma_start(stored[:, 0:C1], result[:, 0:C1])
 
         gather(0)
         flip(0)

@@ -38,14 +38,15 @@ def tile_forestclf_b_kernel(tc, d, wc, bc, w1, b1, w2, b2, offs, out):
         one = held.tile([P, 1], F32, name="one")
         nc.scalar.activation(one[:], zero[:], ACT.Exp)
 
-        offsets = held.tile([P, T * F // 16], U16, name="offsets")
-        nc.sync.dma_start(offsets[:], offs)
-
         window = {}
 
         def load_window(i):
             window[i] = windows.tile([P, S], F32, name="window")
             nc.sync.dma_start(window[i][:], d[i * P : (i + 1) * P, :])
+
+        load_window(0)
+        offsets = held.tile([P, T * F // 16], U16, name="offsets")
+        nc.sync.dma_start(offsets[:], offs)
 
         w1c = held.tile([P, T, KF, W1_ROW], BF16, name="w1c")
         b1c = held.tile([P, T, B1_ROW], F32, name="b1c")
@@ -74,7 +75,6 @@ def tile_forestclf_b_kernel(tc, d, wc, bc, w1, b1, w2, b2, offs, out):
         nc.sync.dma_start(wc_dense[:], wc.rearrange("t (p a) e -> p t a e", a=KF))
         nc.vector.tensor_copy(w1c[:, :, :, C1:HZ], wc_dense[:])
 
-        load_window(0)
         load_hidden_weights(0)
         load_window(1)
         load_wide_weights(0, range(0, KF + KH))
@@ -150,8 +150,8 @@ def tile_forestclf_b_kernel(tc, d, wc, bc, w1, b1, w2, b2, offs, out):
                         u_bank[k, n][:], lhsT=stationary, rhs=w2_rows[t, a][:, n * BANK : (n + 1) * BANK],
                         start=(a == 0), stop=(a == KF + KH - 1),
                     )
-                if a % 2 == 0 and a < KF and live(k + 2):
-                    flip_block(k + 2, a // 2)
+                if a == KF // 2 - 1 and live(k + 2):
+                    flip(k + 2)
 
         def softmax_sum(k, col, values):
             nc.vector.tensor_reduce(neg_max[k][:, col : col + 1], values, X_AXIS, ALU.max, negate=True)

@@ -20,6 +20,8 @@ B1_ROW = C1 + 8
 H_COL, U_COL, Z_COL = 0, 1, 2
 LN2 = 0.6931471805599453
 GUESS_SCALE, GUESS_SHIFT = LN2 / 2.0**23, (0.0861 / 2.0 - 127.0) * LN2
+BLOCKS_BEFORE_FLIPS = 3
+BLOCKS_BEFORE_HIDDEN = 5
 
 FLOPS = 2 * B * T * (F * (E + C1 + C2) + C1 * C2)
 
@@ -58,14 +60,12 @@ def tile_forestclf_b_kernel(tc, d, wc, bc, w1, b1, w2, b2, offs, out):
             nc.sync.dma_start(b1c[:, t, 0:C1], b1[t, :].partition_broadcast(P))
             nc.sync.dma_start(b1c[:, t, C1:HZ], bc[t, :].partition_broadcast(P))
 
-        def load_wide_weights(t, row_blocks):
+        def load_wide_weights(t):
             feature_rows = w2[t, 0:F, :].rearrange("(p a) k -> a p k", a=KF)
             hidden_rows = w2[t, F : F + C1, :].rearrange("(p a) k -> a p k", a=KH)
-            for a in row_blocks:
+            for a in range(KF + KH):
                 w2_rows[t, a] = held.tile([P, C2], BF16, name="w2_rows_%d_%d" % (t, a))
                 nc.sync.dma_start(w2_rows[t, a][:], feature_rows[a, :, :] if a < KF else hidden_rows[a - KF, :, :])
-
-        def load_wide_bias(t):
             nc.sync.dma_start(b2_all[:, t, :], b2[t, :].partition_broadcast(P))
 
         identity = held.tile([P, P], F32, name="identity")
@@ -77,12 +77,10 @@ def tile_forestclf_b_kernel(tc, d, wc, bc, w1, b1, w2, b2, offs, out):
 
         load_hidden_weights(0)
         load_window(1)
-        load_wide_weights(0, range(0, KF + KH))
-        load_wide_bias(0)
+        load_wide_weights(0)
         load_window(2)
         load_hidden_weights(1)
-        load_wide_weights(1, range(0, KF + KH))
-        load_wide_bias(1)
+        load_wide_weights(1)
 
         rounded, flip_bank, flipped, h_bank, hz, relu, relu_bank, relu_flipped = {}, {}, {}, {}, {}, {}, {}, {}
         u_bank, u_biased, neg_max, exp_sum, inverse, log_base = {}, {}, {}, {}, {}, {}
@@ -105,17 +103,12 @@ def tile_forestclf_b_kernel(tc, d, wc, bc, w1, b1, w2, b2, offs, out):
             if t == T - 1 and i + WINDOWS < B // P:
                 load_window(i + WINDOWS)
 
-        def flip_block(k, g):
-            if g == 0:
-                flip_bank[k] = psum_double.tile([P, KF // 2, P], F32, name="flip_bank")
-            nc.tensor.transpose(flip_bank[k][:, g, :], rounded[k][:].bitcast(F32)[:, g : F // 2 : KF // 2], identity[:])
-            if g == KF // 2 - 1:
-                flipped[k] = work.tile([P, KF // 2, 2 * P], BF16, name="flipped")
-                nc.scalar.copy(flipped[k][:], flip_bank[k][:].bitcast(BF16))
-
         def flip(k):
+            flip_bank[k] = psum_double.tile([P, KF // 2, P], F32, name="flip_bank")
             for g in range(KF // 2):
-                flip_block(k, g)
+                nc.tensor.transpose(flip_bank[k][:, g, :], rounded[k][:].bitcast(F32)[:, g : F // 2 : KF // 2], identity[:])
+            flipped[k] = work.tile([P, KF // 2, 2 * P], BF16, name="flipped")
+            nc.scalar.copy(flipped[k][:], flip_bank[k][:].bitcast(BF16))
 
         def feature_block(k, a):
             return flipped[k][:, a // 2, a % 2 : 2 * P : 2]
@@ -150,8 +143,6 @@ def tile_forestclf_b_kernel(tc, d, wc, bc, w1, b1, w2, b2, offs, out):
                         u_bank[k, n][:], lhsT=stationary, rhs=w2_rows[t, a][:, n * BANK : (n + 1) * BANK],
                         start=(a == 0), stop=(a == KF + KH - 1),
                     )
-                if a == KF // 2 - 1 and live(k + 2):
-                    flip(k + 2)
 
         def softmax_sum(k, col, values):
             nc.vector.tensor_reduce(neg_max[k][:, col : col + 1], values, X_AXIS, ALU.max, negate=True)
@@ -216,15 +207,18 @@ def tile_forestclf_b_kernel(tc, d, wc, bc, w1, b1, w2, b2, offs, out):
             if live(k):
                 for n in range(C2 // BANK):
                     u_bank[k, n] = psum_double.tile([P, BANK], F32, name="u_bank_%d" % n)
-                wide_product(k, range(0, KF // 2))
+                wide_product(k, range(0, BLOCKS_BEFORE_FLIPS))
                 flip_relu(k)
                 copy_flipped_relu(k)
-                wide_product(k, range(KF // 2, KF))
+            if live(k + 2):
+                flip(k + 2)
+            if live(k):
+                wide_product(k, range(BLOCKS_BEFORE_FLIPS, BLOCKS_BEFORE_HIDDEN))
             if live(k + 1):
                 hidden_product(k + 1)
                 hidden_bias(k + 1)
             if live(k):
-                wide_product(k, range(KF, KF + KH))
+                wide_product(k, range(BLOCKS_BEFORE_HIDDEN, KF + KH))
             if live(k - 1):
                 wide_bias(k - 1)
             if live(k - 2):

@@ -56,24 +56,26 @@ def tile_forestclf_b_kernel(tc, d, wc, bc, w1, b1, w2, b2, offs, out):
         w2_rows = {}
 
         def load_hidden_weights(t):
-            nc.sync.dma_start(w1c[:, t, :, 0:C1], w1[t, :, :].rearrange("(p a) c -> p a c", a=KF))
+            for g in range(KF // 2):
+                two_rows = w1[t, 2 * g * P : 2 * (g + 1) * P, :].rearrange("(p r) c -> p r c", r=2)
+                nc.sync.dma_start(w1c[:, t, 2 * g : 2 * g + 2, 0:C1], two_rows)
             nc.sync.dma_start(b1c[:, t, 0:C1], b1[t, :].partition_broadcast(P))
             nc.sync.dma_start(b1c[:, t, C1:HZ], bc[t, :].partition_broadcast(P))
 
         def load_wide_weights(t):
-            feature_rows = w2[t, 0:F, :].rearrange("(p a) k -> a p k", a=KF)
+            feature_rows = w2[t, 0:F, :].rearrange("(g p r) k -> g r p k", p=P, r=2)
             hidden_rows = w2[t, F : F + C1, :].rearrange("(p a) k -> a p k", a=KH)
             for a in range(KF + KH):
                 w2_rows[t, a] = held.tile([P, C2], BF16, name="w2_rows_%d_%d" % (t, a))
-                nc.sync.dma_start(w2_rows[t, a][:], feature_rows[a, :, :] if a < KF else hidden_rows[a - KF, :, :])
+                nc.sync.dma_start(w2_rows[t, a][:], feature_rows[a // 2, a % 2, :, :] if a < KF else hidden_rows[a - KF, :, :])
             nc.sync.dma_start(b2_all[:, t, :], b2[t, :].partition_broadcast(P))
 
         identity = held.tile([P, P], F32, name="identity")
         make_identity(nc, identity[:])
 
-        wc_dense = held.tile([P, T, KF, E], BF16, name="wc_dense")
-        nc.sync.dma_start(wc_dense[:], wc.rearrange("t (p a) e -> p t a e", a=KF))
-        nc.vector.tensor_copy(w1c[:, :, :, C1:HZ], wc_dense[:])
+        wc_dense = held.tile([P, T, KF // 2, 2 * E], BF16, name="wc_dense")
+        nc.sync.dma_start(wc_dense[:], wc.rearrange("t (g p r) e -> p t g (r e)", p=P, r=2))
+        nc.vector.tensor_copy(w1c[:, :, :, C1:HZ], wc_dense[:].rearrange("p t g (r e) -> p t (g r) e", e=E))
 
         load_hidden_weights(0)
         load_window(1)
@@ -106,7 +108,7 @@ def tile_forestclf_b_kernel(tc, d, wc, bc, w1, b1, w2, b2, offs, out):
         def flip(k):
             flip_bank[k] = psum_double.tile([P, KF // 2, P], F32, name="flip_bank")
             for g in range(KF // 2):
-                nc.tensor.transpose(flip_bank[k][:, g, :], rounded[k][:].bitcast(F32)[:, g : F // 2 : KF // 2], identity[:])
+                nc.tensor.transpose(flip_bank[k][:, g, :], rounded[k][:].bitcast(F32)[:, g * P : (g + 1) * P], identity[:])
             flipped[k] = work.tile([P, KF // 2, 2 * P], BF16, name="flipped")
             nc.scalar.copy(flipped[k][:], flip_bank[k][:].bitcast(BF16))
 

@@ -53,7 +53,7 @@ def tile_forestclf_b_kernel(tc, d, wc, bc, w1, b1, w2, b2, offs, out):
         w1c = held.tile([P, T, KF, W1_ROW], BF16, name="w1c")
         b1c = held.tile([P, T, B1_ROW], F32, name="b1c")
         b2_all = held.tile([P, T, C2], F32, name="b2_all")
-        w2_rows = {}
+        w2_pair = {}
 
         def load_hidden_weights(t):
             for g in range(KF // 2):
@@ -63,11 +63,10 @@ def tile_forestclf_b_kernel(tc, d, wc, bc, w1, b1, w2, b2, offs, out):
             nc.sync.dma_start(b1c[:, t, C1:HZ], bc[t, :].partition_broadcast(P))
 
         def load_wide_weights(t):
-            feature_rows = w2[t, 0:F, :].rearrange("(g p r) k -> g r p k", p=P, r=2)
-            hidden_rows = w2[t, F : F + C1, :].rearrange("(p a) k -> a p k", a=KH)
-            for a in range(KF + KH):
-                w2_rows[t, a] = held.tile([P, C2], BF16, name="w2_rows_%d_%d" % (t, a))
-                nc.sync.dma_start(w2_rows[t, a][:], feature_rows[a // 2, a % 2, :, :] if a < KF else hidden_rows[a - KF, :, :])
+            row_pairs = w2[t, :, :].rearrange("(g p r) k -> g p r k", p=P, r=2)
+            for g in range((KF + KH) // 2):
+                w2_pair[t, g] = held.tile([P, 2, C2], BF16, name="w2_pair_%d_%d" % (t, g))
+                nc.sync.dma_start(w2_pair[t, g][:], row_pairs[g, :, :, :])
             nc.sync.dma_start(b2_all[:, t, :], b2[t, :].partition_broadcast(P))
 
         identity = held.tile([P, P], F32, name="identity")
@@ -142,7 +141,7 @@ def tile_forestclf_b_kernel(tc, d, wc, bc, w1, b1, w2, b2, offs, out):
                 stationary = feature_block(k, a) if a < KF else relu_flipped[k][:, a - KF : KH * P : KH]
                 for n in range(C2 // BANK):
                     nc.tensor.matmul(
-                        u_bank[k, n][:], lhsT=stationary, rhs=w2_rows[t, a][:, n * BANK : (n + 1) * BANK],
+                        u_bank[k, n][:], lhsT=stationary, rhs=w2_pair[t, a // 2][:, a % 2, n * BANK : (n + 1) * BANK],
                         start=(a == 0), stop=(a == KF + KH - 1),
                     )
 

@@ -12,7 +12,7 @@ UNITS = (B // P) * T
 KF = F // P
 KH = C1 // P
 BANK = 512
-WINDOWS = 3
+WINDOWS = 4
 HZ = C1 + E
 WIDTH = C1 + C2
 W1_ROW = C1 + 16
@@ -62,11 +62,13 @@ def tile_forestclf_b_kernel(tc, d, wc, bc, w1, b1, w2, b2, offs, out):
             nc.sync.dma_start(b1c[:, t, 0:C1], b1[t, :].partition_broadcast(P))
             nc.sync.dma_start(b1c[:, t, C1:HZ], bc[t, :].partition_broadcast(P))
 
-        def load_wide_weights(t):
+        def load_wide_weights(t, pairs):
             row_pairs = w2[t, :, :].rearrange("(g p r) k -> g p r k", p=P, r=2)
-            for g in range((KF + KH) // 2):
+            for g in pairs:
                 w2_pair[t, g] = held.tile([P, 2, C2], BF16, name="w2_pair_%d_%d" % (t, g))
                 nc.sync.dma_start(w2_pair[t, g][:], row_pairs[g, :, :, :])
+
+        def load_wide_bias(t):
             nc.sync.dma_start(b2_all[:, t, :], b2[t, :].partition_broadcast(P))
 
         identity = held.tile([P, P], F32, name="identity")
@@ -78,10 +80,14 @@ def tile_forestclf_b_kernel(tc, d, wc, bc, w1, b1, w2, b2, offs, out):
 
         load_hidden_weights(0)
         load_window(1)
-        load_wide_weights(0)
-        load_window(2)
+        load_wide_weights(0, (0, 1, 2, 3))
         load_hidden_weights(1)
-        load_wide_weights(1)
+        load_wide_bias(0)
+        load_window(2)
+        load_wide_weights(1, (0, 1))
+        load_window(3)
+        load_wide_weights(1, (2, 3))
+        load_wide_bias(1)
 
         rounded, flip_bank, flipped, h_bank, hz, relu, relu_bank, relu_flipped = {}, {}, {}, {}, {}, {}, {}, {}
         u_bank, u_biased, neg_max, exp_sum, inverse, log_base = {}, {}, {}, {}, {}, {}

@@ -82,8 +82,8 @@ def tile_forestclf_b_kernel(tc, d, wc, bc, w1, b1, w2, b2, offs, out):
         load_window(1)
         load_wide_weights(0, (0, 1, 2, 3))
         load_hidden_weights(1)
-        load_wide_bias(0)
         load_window(2)
+        load_wide_bias(0)
         load_wide_weights(1, (0, 1))
         load_window(3)
         load_wide_weights(1, (2, 3))

@@ -59,6 +59,8 @@ def tile_forestclf_b_kernel(tc, d, wc, bc, w1, b1, w2, b2, offs, out):
             for g in range(KF // 2):
                 two_rows = w1[t, 2 * g * P : 2 * (g + 1) * P, :].rearrange("(p r) c -> p r c", r=2)
                 nc.sync.dma_start(w1c[:, t, 2 * g : 2 * g + 2, 0:C1], two_rows)
+
+        def load_hidden_bias(t):
             nc.sync.dma_start(b1c[:, t, 0:C1], b1[t, :].partition_broadcast(P))
             nc.sync.dma_start(b1c[:, t, C1:HZ], bc[t, :].partition_broadcast(P))
 
@@ -80,8 +82,10 @@ def tile_forestclf_b_kernel(tc, d, wc, bc, w1, b1, w2, b2, offs, out):
 
         load_hidden_weights(0)
         load_window(1)
+        load_hidden_bias(0)
         load_wide_weights(0, (0, 1, 2, 3))
         load_hidden_weights(1)
+        load_hidden_bias(1)
         load_window(2)
         load_wide_bias(0)
         load_wide_weights(1, (0, 1))

@@ -179,12 +179,14 @@ def tile_forestclf_b_kernel(tc, d, wc, bc, w1, b1, w2, b2, offs, out):
         def log_guess(k):
             inverse[k] = work.tile([P, 3], F32, name="inverse")
             nc.scalar.activation(inverse[k][:], exp_sum[k][:].bitcast(U32), ACT.Exp, scale=-GUESS_SCALE, bias=-GUESS_SHIFT)
-            guess = work.tile([P, 3], F32, name="guess")
-            nc.vector.tensor_scalar(guess[:], exp_sum[k][:].bitcast(I32), GUESS_SCALE, GUESS_SHIFT, ALU.mult, ALU.add)
             log_base[k] = work.tile([P, 3], F32, name="log_base")
-            nc.vector.scalar_tensor_tensor(log_base[k][:], guess[:], -1.5, neg_max[k][:], ALU.add, ALU.subtract)
+            nc.vector.scalar_tensor_tensor(
+                log_base[k][:], exp_sum[k][:].bitcast(I32), GUESS_SCALE, neg_max[k][:], ALU.mult, ALU.subtract
+            )
             z_base = log_base[k][:, Z_COL : Z_COL + 1]
-            nc.vector.tensor_tensor(z_base, z_base, hz[k][:, C1 + 1 : C1 + 2], ALU.subtract)
+            nc.vector.scalar_tensor_tensor(
+                z_base, z_base, 2.0 * (GUESS_SHIFT - 1.5), hz[k][:, C1 + 1 : C1 + 2], ALU.add, ALU.subtract
+            )
 
         def finish(k):
             i, t = block_and_tree(k)

@@ -46,6 +46,8 @@ def tile_forestclf_b_kernel(tc, d, wc, bc, w1, b1, w2, b2, offs, out):
             window[i] = windows.tile([P, S], F32, name="window")
             nc.sync.dma_start(window[i][:], d[i * P : (i + 1) * P, :])
 
+        bias_row = held.tile([1, C2], F32, name="bias_row")
+        nc.sync.dma_start(bias_row[:], b2[0:1, :])
         load_window(0)
         offsets = held.tile([P, T * F // 16], U16, name="offsets")
         nc.sync.dma_start(offsets[:], offs)
@@ -87,11 +89,18 @@ def tile_forestclf_b_kernel(tc, d, wc, bc, w1, b1, w2, b2, offs, out):
         load_hidden_weights(1)
         load_hidden_bias(1)
         load_window(2)
-        load_wide_bias(0)
         load_wide_weights(1, (0, 1))
         load_window(3)
         load_wide_weights(1, (2, 3))
         load_wide_bias(1)
+
+        ones_row = held.tile([1, P], F32, name="ones_row")
+        nc.vector.memset(ones_row[:], 1.0)
+        for n in range(C2 // BANK):
+            cols = slice(n * BANK, (n + 1) * BANK)
+            spread = psum_double.tile([P, BANK], F32, name="u_bank_%d" % n)
+            nc.tensor.matmul(spread[:], lhsT=ones_row[:], rhs=bias_row[:, cols], start=True, stop=True)
+            nc.vector.tensor_copy(b2_all[:, 0, cols], spread[:])
 
         rounded, flip_bank, flipped, h_bank, hz, relu, relu_bank, relu_flipped = {}, {}, {}, {}, {}, {}, {}, {}
         u_bank, u_biased, neg_max, exp_sum, inverse, log_base = {}, {}, {}, {}, {}, {}

@@ -123,12 +123,12 @@ def tile_forestclf_b_kernel(tc, d, wc, bc, w1, b1, w2, b2, offs, out):
             if t == T - 1 and i + WINDOWS < B // P:
                 load_window(i + WINDOWS)
 
-        def flip(k):
+        def flip(k, copy_out):
             flip_bank[k] = psum_double.tile([P, KF // 2, P], F32, name="flip_bank")
             for g in range(KF // 2):
                 nc.tensor.transpose(flip_bank[k][:, g, :], rounded[k][:].bitcast(F32)[:, g * P : (g + 1) * P], identity[:])
             flipped[k] = work.tile([P, KF // 2, 2 * P], BF16, name="flipped")
-            nc.scalar.copy(flipped[k][:], flip_bank[k][:].bitcast(BF16))
+            copy_out(flipped[k][:], flip_bank[k][:].bitcast(BF16))
 
         def feature_block(k, a):
             return flipped[k][:, a // 2, a % 2 : 2 * P : 2]
@@ -218,12 +218,12 @@ def tile_forestclf_b_kernel(tc, d, wc, bc, w1, b1, w2, b2, offs, out):
             nc.sync.dma_start(stored[:, 0:C1], result[:, 0:C1])
 
         gather(0)
-        flip(0)
+        flip(0, nc.vector.tensor_copy)
         hidden_product(0)
         hidden_bias(0)
         gather(2)
         gather(1)
-        flip(1)
+        flip(1, nc.scalar.copy)
         gather(3)
         for k in range(UNITS + 2):
             if live(k):
@@ -233,7 +233,7 @@ def tile_forestclf_b_kernel(tc, d, wc, bc, w1, b1, w2, b2, offs, out):
                 flip_relu(k)
                 copy_flipped_relu(k)
             if live(k + 2):
-                flip(k + 2)
+                flip(k + 2, nc.scalar.copy)
             if live(k):
                 wide_product(k, range(BLOCKS_BEFORE_FLIPS, BLOCKS_BEFORE_HIDDEN))
             if live(k + 1):

import concourse.mybir as mybir
from concourse.masks import make_identity

F32, BF16, U16, I32, U32 = mybir.dt.float32, mybir.dt.bfloat16, mybir.dt.uint16, mybir.dt.int32, mybir.dt.uint32
ACT = mybir.ActivationFunctionType
ALU = mybir.AluOpType
X_AXIS = mybir.AxisListType.X

P = 128
B, S, T, F, E, C1, C2 = 1024, 2048, 2, 768, 2, 256, 1024
UNITS = (B // P) * T
KF = F // P
KH = C1 // P
BANK = 512
WINDOWS = 4
HZ = C1 + E
WIDTH = C1 + C2
W1_ROW = C1 + 16
B1_ROW = C1 + 8
H_COL, U_COL, Z_COL = 0, 1, 2
LN2 = 0.6931471805599453
GUESS_SCALE, GUESS_SHIFT = LN2 / 2.0**23, (0.0861 / 2.0 - 127.0) * LN2
BLOCKS_BEFORE_FLIPS = 3
BLOCKS_BEFORE_HIDDEN = 5

FLOPS = 2 * B * T * (F * (E + C1 + C2) + C1 * C2)


def tile_forestclf_b_kernel(tc, d, wc, bc, w1, b1, w2, b2, offs, out):
    nc = tc.nc
    with (
        tc.tile_pool(name="held", bufs=1) as held,
        tc.tile_pool(name="windows", bufs=WINDOWS) as windows,
        tc.tile_pool(name="work", bufs=4) as work,
        tc.psum_pool(name="psum_single", bufs=1) as psum_single,
        tc.psum_pool(name="psum_double", bufs=2) as psum_double,
    ):
        zero = held.tile([P, 1], F32, name="zero")
        nc.vector.memset(zero[:], 0.0)
        one = held.tile([P, 1], F32, name="one")
        nc.scalar.activation(one[:], zero[:], ACT.Exp)

        window = {}

        def load_window(i):
            window[i] = windows.tile([P, S], F32, name="window")
            nc.sync.dma_start(window[i][:], d[i * P : (i + 1) * P, :])

        bias_row = held.tile([1, C2], F32, name="bias_row")
        nc.sync.dma_start(bias_row[:], b2[0:1, :])
        load_window(0)
        offsets = held.tile([P, T * F // 16], U16, name="offsets")
        nc.sync.dma_start(offsets[:], offs)

        w1c = held.tile([P, T, KF, W1_ROW], BF16, name="w1c")
        b1c = held.tile([P, T, B1_ROW], F32, name="b1c")
        b2_all = held.tile([P, T, C2], F32, name="b2_all")
        w2_pair = {}

        def load_hidden_weights(t):
            for g in range(KF // 2):
                two_rows = w1[t, 2 * g * P : 2 * (g + 1) * P, :].rearrange("(p r) c -> p r c", r=2)
                nc.sync.dma_start(w1c[:, t, 2 * g : 2 * g + 2, 0:C1], two_rows)

        def load_hidden_bias(t):
            nc.sync.dma_start(b1c[:, t, 0:C1], b1[t, :].partition_broadcast(P))
            nc.sync.dma_start(b1c[:, t, C1:HZ], bc[t, :].partition_broadcast(P))

        def load_wide_weights(t, pairs):
            row_pairs = w2[t, :, :].rearrange("(g p r) k -> g p r k", p=P, r=2)
            for g in pairs:
                w2_pair[t, g] = held.tile([P, 2, C2], BF16, name="w2_pair_%d_%d" % (t, g))
                nc.sync.dma_start(w2_pair[t, g][:], row_pairs[g, :, :, :])

        def load_wide_bias(t):
            nc.sync.dma_start(b2_all[:, t, :], b2[t, :].partition_broadcast(P))

        identity = held.tile([P, P], F32, name="identity")
        make_identity(nc, identity[:])

        wc_dense = held.tile([P, T, KF // 2, 2 * E], BF16, name="wc_dense")
        nc.sync.dma_start(wc_dense[:], wc.rearrange("t (g p r) e -> p t g (r e)", p=P, r=2))
        nc.vector.tensor_copy(w1c[:, :, :, C1:HZ], wc_dense[:].rearrange("p t g (r e) -> p t (g r) e", e=E))

        load_hidden_weights(0)
        load_window(1)
        load_hidden_bias(0)
        load_wide_weights(0, (0, 1, 2, 3))
        load_hidden_weights(1)
        load_hidden_bias(1)
        load_window(2)
        load_wide_weights(1, (0, 1))
        load_window(3)
        load_wide_weights(1, (2, 3))
        load_wide_bias(1)

        ones_row = held.tile([1, P], F32, name="ones_row")
        nc.vector.memset(ones_row[:], 1.0)
        for n in range(C2 // BANK):
            cols = slice(n * BANK, (n + 1) * BANK)
            spread = psum_double.tile([P, BANK], F32, name="u_bank_%d" % n)
            nc.tensor.matmul(spread[:], lhsT=ones_row[:], rhs=bias_row[:, cols], start=True, stop=True)
            nc.vector.tensor_copy(b2_all[:, 0, cols], spread[:])

        rounded, flip_bank, flipped, h_bank, hz, relu, relu_bank, relu_flipped = {}, {}, {}, {}, {}, {}, {}, {}
        u_bank, u_biased, neg_max, exp_sum, inverse, log_base = {}, {}, {}, {}, {}, {}

        def live(j):
            return 0 <= j < UNITS

        def block_and_tree(k):
            group, rest = divmod(k, 2 * T)
            t, j = divmod(rest, 2)
            return 2 * group + j, t

        def gather(k):
            i, t = block_and_tree(k)
            picked = work.tile([P, F], F32, name="picked")
            piece = offsets[:, t * (F // 16) : (t + 1) * (F // 16)]
            nc.scalar.activation(picked[:], window[i][:].indirect(piece), ACT.Copy)
            rounded[k] = work.tile([P, F], BF16, name="rounded")
            nc.vector.tensor_copy(rounded[k][:], picked[:])
            if t == T - 1 and i + WINDOWS < B // P:
                load_window(i + WINDOWS)

        def flip(k, copy_out):
            flip_bank[k] = psum_double.tile([P, KF // 2, P], F32, name="flip_bank")
            for g in range(KF // 2):
                nc.tensor.transpose(flip_bank[k][:, g, :], rounded[k][:].bitcast(F32)[:, g * P : (g + 1) * P], identity[:])
            flipped[k] = work.tile([P, KF // 2, 2 * P], BF16, name="flipped")
            copy_out(flipped[k][:], flip_bank[k][:].bitcast(BF16))

        def feature_block(k, a):
            return flipped[k][:, a // 2, a % 2 : 2 * P : 2]

        def hidden_product(k):
            t = block_and_tree(k)[1]
            h_bank[k] = psum_single.tile([P, HZ], F32, name="h_bank")
            for a in range(KF):
                nc.tensor.matmul(h_bank[k][:], lhsT=feature_block(k, a), rhs=w1c[:, t, a, 0:HZ], start=(a == 0), stop=(a == KF - 1))

        def hidden_bias(k):
            t = block_and_tree(k)[1]
            hz[k] = work.tile([P, HZ], F32, name="hz")
            nc.vector.tensor_tensor(hz[k][:], h_bank[k][:], b1c[:, t, 0:HZ], ALU.add)
            relu[k] = work.tile([P, C1], BF16, name="relu")
            nc.vector.tensor_scalar_max(relu[k][:], hz[k][:, 0:C1], 0.0)

        def flip_relu(k):
            relu_bank[k] = psum_single.tile([P, P], F32, name="relu_bank")
            nc.tensor.transpose(relu_bank[k][:], relu[k][:].bitcast(F32), identity[:])

        def copy_flipped_relu(k):
            relu_flipped[k] = work.tile([P, KH * P], BF16, name="relu_flipped")
            nc.vector.tensor_copy(relu_flipped[k][:], relu_bank[k][:].bitcast(BF16))

        def wide_product(k, row_blocks):
            t = block_and_tree(k)[1]
            for a in row_blocks:
                stationary = feature_block(k, a) if a < KF else relu_flipped[k][:, a - KF : KH * P : KH]
                for n in range(C2 // BANK):
                    nc.tensor.matmul(
                        u_bank[k, n][:], lhsT=stationary, rhs=w2_pair[t, a // 2][:, a % 2, n * BANK : (n + 1) * BANK],
                        start=(a == 0), stop=(a == KF + KH - 1),
                    )

        def softmax_sum(k, col, values):
            nc.vector.tensor_reduce(neg_max[k][:, col : col + 1], values, X_AXIS, ALU.max, negate=True)
            unused = work.tile([P, C2], BF16, name="unused")
            nc.scalar.activation(
                unused[:, 0 : values.shape[1]], values, ACT.Exp,
                bias=neg_max[k][:, col : col + 1], accum_out=exp_sum[k][:, col : col + 1],
            )

        def hidden_softmax_sums(k):
            neg_max[k] = work.tile([P, 3], F32, name="neg_max")
            exp_sum[k] = work.tile([P, 3], F32, name="exp_sum")
            softmax_sum(k, H_COL, hz[k][:, 0:C1])
            softmax_sum(k, Z_COL, hz[k][:, C1:HZ])

        def wide_bias(k):
            t = block_and_tree(k)[1]
            u_biased[k] = work.tile([P, C2], F32, name="u_biased")
            for n in range(C2 // BANK):
                cols = slice(n * BANK, (n + 1) * BANK)
                nc.vector.tensor_tensor(u_biased[k][:, cols], u_bank[k, n][:], b2_all[:, t, cols], ALU.add)

        def log_guess(k):
            inverse[k] = work.tile([P, 3], F32, name="inverse")
            nc.scalar.activation(inverse[k][:], exp_sum[k][:].bitcast(U32), ACT.Exp, scale=-GUESS_SCALE, bias=-GUESS_SHIFT)
            log_base[k] = work.tile([P, 3], F32, name="log_base")
            nc.vector.scalar_tensor_tensor(
                log_base[k][:], exp_sum[k][:].bitcast(I32), GUESS_SCALE, neg_max[k][:], ALU.mult, ALU.subtract
            )
            z_base = log_base[k][:, Z_COL : Z_COL + 1]
            nc.vector.scalar_tensor_tensor(
                z_base, z_base, 2.0 * (GUESS_SHIFT - 1.5), hz[k][:, C1 + 1 : C1 + 2], ALU.add, ALU.subtract
            )

        def finish(k):
            i, t = block_and_tree(k)
            neg_half = work.tile([P, 3], F32, name="neg_half")
            nc.vector.scalar_tensor_tensor(neg_half[:], inverse[k][:], -0.5, exp_sum[k][:], ALU.mult, ALU.mult)
            product = work.tile([P, 3], F32, name="product")
            nc.vector.scalar_tensor_tensor(product[:], neg_half[:], 2.0, neg_half[:], ALU.add, ALU.mult)
            log_norm = work.tile([P, 3], F32, name="log_norm")
            nc.vector.scalar_tensor_tensor(log_norm[:], product[:], -2.0, log_base[k][:], ALU.mult, ALU.add)
            neg_lw = log_norm[:, Z_COL : Z_COL + 1]
            result = work.tile([P, WIDTH], F32, name="result")
            stored = out[i * P : (i + 1) * P, t * WIDTH : (t + 1) * WIDTH]
            nc.vector.tensor_scalar(
                result[:, C1:WIDTH], u_biased[k][:], log_norm[:, U_COL : U_COL + 1], neg_lw, ALU.subtract, ALU.subtract
            )
            nc.sync.dma_start(stored[:, C1:WIDTH], result[:, C1:WIDTH])
            nc.vector.tensor_scalar(
                result[:, 0:C1], hz[k][:, 0:C1], log_norm[:, H_COL : H_COL + 1], neg_lw, ALU.subtract, ALU.subtract
            )
            nc.sync.dma_start(stored[:, 0:C1], result[:, 0:C1])

        gather(0)
        flip(0, nc.vector.tensor_copy)
        hidden_product(0)
        hidden_bias(0)
        gather(2)
        gather(1)
        flip(1, nc.scalar.copy)
        gather(3)
        for k in range(UNITS + 2):
            if live(k):
                for n in range(C2 // BANK):
                    u_bank[k, n] = psum_double.tile([P, BANK], F32, name="u_bank_%d" % n)
                wide_product(k, range(0, BLOCKS_BEFORE_FLIPS))
                flip_relu(k)
                copy_flipped_relu(k)
            if live(k + 2):
                flip(k + 2, nc.scalar.copy)
            if live(k):
                wide_product(k, range(BLOCKS_BEFORE_FLIPS, BLOCKS_BEFORE_HIDDEN))
            if live(k + 1):
                hidden_product(k + 1)
                hidden_bias(k + 1)
            if live(k):
                wide_product(k, range(BLOCKS_BEFORE_HIDDEN, KF + KH))
            if live(k - 1):
                wide_bias(k - 1)
            if live(k - 2):
                log_guess(k - 2)
            if live(k - 1):
                softmax_sum(k - 1, U_COL, u_biased[k - 1][:])
            if live(k):
                hidden_softmax_sums(k)
            if live(k + 4):
                gather(k + 4)
            if live(k - 2):
                finish(k - 2)
